import numpy as np
import ml_dtypes


def mxq(x, axis, fmt="e4m3"):
    dtype, down = {"e4m3": (ml_dtypes.float8_e4m3fn, 7), "e5m2": (ml_dtypes.float8_e5m2, 14)}[fmt]
    v = np.moveaxis(np.asarray(x, np.float32).astype(ml_dtypes.bfloat16).astype(np.float64), axis, -1)
    blocks = v.reshape(v.shape[:-1] + (-1, 32))
    amax = np.abs(blocks).max(-1, keepdims=True)
    byte = np.maximum(np.where(amax > 0, np.frexp(amax)[1] - 1 + 127, 0) - down, 1)
    scale = np.exp2(byte - 127.0)
    codes = (blocks / scale).astype(np.float32).astype(dtype).astype(np.float64)
    return np.moveaxis((codes * scale).reshape(v.shape), -1, axis)


WIDE = False


def mx_kscale(k):
    if not WIDE:
        return np.ones(k)
    levels = np.array([10, -10, 5, -5, 0])
    if k % 512:
        return np.exp2(np.random.permutation(np.resize(levels, k // 32))).repeat(32)
    a = np.empty((k // 512, 16))
    for p in range(k // 512):
        a[p, :8] = np.random.permutation(np.resize(levels, 8))
        for g in range(8):
            far = levels[np.abs(levels - a[p, g]) >= 10]
            a[p, g + 8] = far[np.random.randint(len(far))]
    return np.exp2(a.ravel()).repeat(32)


BF16 = ml_dtypes.bfloat16


def bf(x):
    return np.asarray(x, np.float32).astype(BF16)


def f64(x):
    return np.asarray(x).astype(np.float64)


B, T, S, Dt, Df = 8, 1024, 256, 512, 512
EPS = 1e-6


def rmsnorm(x, w):
    return x * (1.0 / np.sqrt(np.mean(x * x, axis=-1, keepdims=True) + EPS)) * w


def draw0():
    s = mx_kscale(Dt)
    t = mx_kscale(Df)
    return {"text": bf(np.random.standard_normal((B, T, Dt)) * s),
            "Wq_w": bf(np.random.standard_normal((Df, Dt)) / np.sqrt(Dt) / s[None, :]),
            "Wq_b": bf(np.random.standard_normal(Df) * 0.3),
            "qn_w": bf((1.0 + 0.1 * np.random.standard_normal(Df)) * t),
            "k_norm": bf(np.random.standard_normal((B, S, Df)) / t)}


def core(text, Wq_w, Wq_b, qn_w, k_norm):
    q = (mxq(f64(text), 2, "e4m3") @ mxq(f64(Wq_w), 1, "e4m3").T) + f64(Wq_b)
    q = rmsnorm(q, f64(qn_w))
    scale = 1.0 / np.sqrt(Df)
    return (mxq(q, 2, "e4m3") @ mxq(f64(k_norm), 2, "e4m3").transpose(0, 2, 1)) * scale


def e4m3fn_bytes(y):
    return np.clip(np.asarray(y, np.float64), -448.0, 448.0).astype(np.float32).astype(ml_dtypes.float8_e4m3fn).view(np.uint8)


def e4m3fn_values(b):
    return np.asarray(b, np.uint8).view(ml_dtypes.float8_e4m3fn).astype(np.float64)


def setup_inputs():
    d = draw0()
    x0 = np.asarray(d['text']).astype(np.float64)
    s = (np.max(np.abs(x0), axis=(0, 1), keepdims=True) / 448.0).astype(np.float32)
    out = {}
    for k, v in d.items():
        if k == 'text':
            out['text_bytes'] = e4m3fn_bytes(x0 / s.astype(np.float64))
            out['text_scale'] = s
        else:
            out[k] = v
    return out


def reference(text_bytes, text_scale, Wq_w, Wq_b, qn_w, k_norm):
    return core(e4m3fn_values(text_bytes) * text_scale.astype(np.float64), Wq_w, Wq_b, qn_w, k_norm)

@@ -1,0 +1,405 @@
+from contextlib import ExitStack
+
+import concourse.mybir as mybir
+from concourse.masks import make_identity
+
+F32 = mybir.dt.float32
+BF16 = mybir.dt.bfloat16
+U32 = mybir.dt.uint32
+U8 = mybir.dt.uint8
+FP8 = mybir.dt.float8_e4m3fn
+FP8X4 = mybir.dt.float8_e4m3fn_x4
+ACT = mybir.ActivationFunctionType
+ALU = mybir.AluOpType
+AX = mybir.AxisListType
+
+B, T, S, D = 8, 1024, 256, 512
+P = 128
+NT = 512
+NB = B * T // NT
+EPS = 1e-6
+FLOPS = 2 * B * T * D * D + 2 * B * T * S * D
+
+
+def tile_crossattention_pb_t_kernel(tc, text_bytes, text_scale, Wq_w, Wq_b, qn_w, k_norm, out):
+    nc = tc.nc
+    xrows = text_bytes.rearrange("b t k -> (b t) k")
+    orows = out.rearrange("b t s -> (b t) s")
+
+    with ExitStack() as ctx:
+        keep = ctx.enter_context(tc.tile_pool(name="keep", bufs=1))
+        raw = ctx.enter_context(tc.tile_pool(name="raw", bufs=1))
+        work = ctx.enter_context(tc.tile_pool(name="work", bufs=2))
+        psum = ctx.enter_context(tc.psum_pool(name="psum", bufs=1))
+        ctx.enter_context(tc.manual_schedule())
+
+        xb = {}
+        kb = {}
+
+        def load_x(i):
+            xb[i] = raw.tile([P, 4, D], U8, name="xbytes", bufs=NB, align_bytes=64)
+            nc.sync.dma_start(out=xb[i][:], in_=xrows[NT * i : NT * (i + 1), :].rearrange("(q j) k -> q j k", j=4))
+
+        def load_k(b):
+            kb[b] = raw.tile([P, 2, D], BF16, name="kraw", bufs=B, align_bytes=64)
+            nc.sync.dma_start(out=kb[b][:], in_=k_norm[b].rearrange("(h q) k -> q h k", q=P))
+
+        scale = keep.tile([P, 2, D], F32, name="scale", align_bytes=64)
+        nc.scalar.dma_start(out=scale[:, 0, :], in_=text_scale.rearrange("a b k -> (a b k)").partition_broadcast(P))
+        load_x(0)
+        b_raw = keep.tile([P, 4], BF16, name="b_raw")
+        nc.scalar.dma_start(out=b_raw[:], in_=Wq_b.rearrange("(p t) -> p t", t=4))
+        g_raw = keep.tile([P, 4], BF16, name="g_raw")
+        nc.scalar.dma_start(out=g_raw[:], in_=qn_w.rearrange("(p t) -> p t", t=4))
+        w_raw = keep.tile([P, 4, D], BF16, name="w_raw", align_bytes=64)
+        nc.sync.dma_start(out=w_raw[:], in_=Wq_w.rearrange("(m t) k -> m t k", t=4))
+        for i in range(1, NB):
+            load_x(i)
+            if i <= B:
+                load_k(i - 1)
+
+        ident = keep.tile([P, P], F32, name="ident", align_bytes=64)
+        make_identity(nc, ident[:])
+        ones = keep.tile([P, 1], F32, name="ones")
+        nc.gpsimd.memset(ones[:], 1.0)
+        neg_half = keep.tile([P, 4], F32, name="neg_half")
+        nc.gpsimd.memset(neg_half[:], -0.5)
+        bias = keep.tile([P, 4], F32, name="bias")
+        gain = keep.tile([P, 4], F32, name="gain")
+        bias_gain = keep.tile([P, 4], F32, name="bias_gain")
+
+        w_codes = keep.tile([P, D], U32, name="w_codes", align_bytes=64)
+        w_scales = keep.tile([P, D], U8, name="w_scales", align_bytes=64)
+        k_codes = keep.tile([P, B, S], U32, name="k_codes", align_bytes=64)
+        k_scales = keep.tile([P, B, S], U8, name="k_scales", align_bytes=64)
+
+        xs = {}
+        xt = {}
+        xg = {}
+        xc = {}
+        q = {}
+        sq = {}
+        z = {}
+        ssum = {}
+        rstd = {}
+        rb = {}
+        y = {}
+        yc = {}
+        ob = {}
+        osb = {}
+        kt = {}
+        kg = {}
+
+        def xp(i, lo, hi):
+            if not 0 <= i < NB:
+                return
+            if lo == 0:
+                xs[i] = work.tile([P, 4 * D], BF16, name="xs", bufs=4, align_bytes=64)
+            bytes_flat = xb[i][:].rearrange("p j k -> p (j k)")
+            scale_flat = scale[:].rearrange("p j k -> p (j k)")
+            nc.vector.tensor_tensor(
+                out=xs[i][:, D * lo : D * hi],
+                in0=bytes_flat[:, D * lo : D * hi].bitcast(FP8),
+                in1=scale_flat[:, 0 : D * (hi - lo)],
+                op=ALU.mult,
+            )
+
+        def xt_half(i, h):
+            if not 0 <= i < NB:
+                return
+            bank = psum.tile([P, 2, 2, P], F32, name="xt", bufs=2)
+            xt[i, h] = bank
+            words = xs[i][:].bitcast(F32)
+            for jj in range(2):
+                j = 2 * h + jj
+                for u in range(2):
+                    nc.tensor.transpose(bank[:, jj, u, :], words[:, 256 * j + u : 256 * (j + 1) : 2], ident[:])
+
+        def xcopy(i, h, eng):
+            if not 0 <= i < NB:
+                return
+            if h == 0:
+                xg[i] = work.tile([P, 4 * NT], BF16, name="xg", bufs=3, align_bytes=64)
+            dst = xg[i][:].bitcast(F32)[:, 512 * h : 512 * (h + 1)].rearrange("p (j q u) -> p j q u", j=2, u=2)
+            src = xt[i, h][:].rearrange("p j u q -> p j q u")
+            if eng == "s":
+                nc.scalar.copy(out=dst, in_=src)
+            else:
+                nc.vector.tensor_copy(out=dst, in_=src)
+
+        def xquant(i):
+            if not 0 <= i < NB:
+                return
+            codes = work.tile([P, NT], U32, name="xcodes", bufs=3, align_bytes=64)
+            scl = work.tile([P, NT], U8, name="xscales", bufs=3, align_bytes=64)
+            xc[i] = (codes, scl)
+            nc.vector.quantize_mx(out=codes[:].bitcast(FP8X4), scales=scl[:], in_=xg[i][:])
+
+        def mm1(i, t):
+            if not 0 <= i < NB:
+                return
+            bank = psum.tile([P, NT], F32, name="q", bufs=4)
+            q[i, t] = bank
+            codes, scl = xc[i]
+            nc.tensor.matmul_mx(
+                out=bank[:],
+                lhsT=w_codes[:, P * t : P * (t + 1)].bitcast(FP8X4),
+                lhsT_scale=w_scales[:, P * t : P * (t + 1)],
+                rhs=codes[:].bitcast(FP8X4),
+                rhs_scale=scl[:],
+                start=True,
+                stop=True,
+            )
+
+        def square(i, t):
+            if not 0 <= i < NB:
+                return
+            if t == 0:
+                sq[i] = work.tile([P, 4, NT], F32, name="sq", bufs=2, align_bytes=64)
+                z[i] = work.tile([P, 4, NT], F32, name="z", bufs=3, align_bytes=64)
+            nc.scalar.activation(out=sq[i][:, t, :], in_=q[i, t][:], func=ACT.Square, bias=bias[:, t : t + 1], scale=1.0)
+
+        def affine(i, t):
+            if not 0 <= i < NB:
+                return
+            nc.scalar.activation(out=z[i][:, t, :], in_=q[i, t][:], func=ACT.Identity, bias=bias_gain[:, t : t + 1], scale=gain[:, t : t + 1])
+
+        def square_and_affine(i, t):
+            square(i, t)
+            affine(i, t)
+
+        def sum_squares(i, h):
+            if not 0 <= i < NB:
+                return
+            if h == 0:
+                ssum[i] = psum.tile([P, 4], F32, name="s", bufs=1)
+            for j in (2 * h, 2 * h + 1):
+                for t in range(4):
+                    nc.tensor.matmul(
+                        out=ssum[i][:, j : j + 1],
+                        lhsT=sq[i][:, t, P * j : P * (j + 1)],
+                        rhs=ones[:],
+                        start=(t == 0),
+                        stop=(t == 3),
+                    )
+
+        def mean_and_rstd(i):
+            if not 0 <= i < NB:
+                return
+            ms = work.tile([P, 4], F32, name="ms", bufs=2)
+            nc.vector.tensor_scalar(out=ms[:], in0=ssum[i][:], scalar1=1.0 / D, scalar2=EPS, op0=ALU.mult, op1=ALU.add)
+            r = work.tile([P, 4], F32, name="rstd", bufs=2)
+            nc.gpsimd.tensor_tensor(out=r[:], in0=ms[:], in1=neg_half[:], op=ALU.pow)
+            rstd[i] = r
+
+        def spread_rstd(i):
+            if not 0 <= i < NB:
+                return
+            bank = psum.tile([P, NT], F32, name="r", bufs=1)
+            rb[i] = bank
+            for j in range(4):
+                nc.tensor.transpose(bank[:, P * j : P * (j + 1)], rstd[i][:, j : j + 1].to_broadcast([P, P]), ident[:])
+
+        def normalise(i, lo=0, hi=NT):
+            if not 0 <= i < NB:
+                return
+            if lo == 0:
+                y[i] = work.tile([P, 4 * NT], BF16, name="y", bufs=2, align_bytes=64)
+            n = hi - lo
+            nc.vector.tensor_tensor(
+                out=y[i][:, 4 * lo : 4 * hi].rearrange("p (c i t) -> p c t i", i=4, t=4),
+                in0=z[i][:, :, lo:hi].rearrange("p t (c i) -> p c t i", i=4),
+                in1=rb[i][:, lo:hi].rearrange("p (c i) -> p c i", i=4).unsqueeze(2).to_broadcast([P, n // 4, 4, 4]),
+                op=ALU.mult,
+            )
+
+        def yquant(i, lo=0, hi=NT):
+            if not 0 <= i < NB:
+                return
+            if lo == 0:
+                codes = work.tile([P, NT], U32, name="ycodes", bufs=2, align_bytes=64)
+                scl = work.tile([P, NT], U8, name="yscales", bufs=2, align_bytes=64)
+                yc[i] = (codes, scl)
+            codes, scl = yc[i]
+            nc.vector.quantize_mx(out=codes[:, lo:hi].bitcast(FP8X4), scales=scl[:, lo:hi], in_=y[i][:, 4 * lo : 4 * hi])
+
+        def mm2(i, h):
+            if not 0 <= i < NB:
+                return
+            b = i // 2
+            codes, scl = yc[i]
+            bank = psum.tile([P, 2, S], F32, name="q", bufs=4)
+            ob[i, h] = bank
+            for jj in range(2):
+                cols = slice(P * (2 * h + jj), P * (2 * h + jj + 1))
+                nc.tensor.matmul_mx(
+                    out=bank[:, jj, :],
+                    lhsT=codes[:, cols].bitcast(FP8X4),
+                    lhsT_scale=scl[:, cols],
+                    rhs=k_codes[:, b, :].bitcast(FP8X4),
+                    rhs_scale=k_scales[:, b, :],
+                    start=True,
+                    stop=True,
+                )
+
+        def ocopy(i, h, eng):
+            if not 0 <= i < NB:
+                return
+            if h == 0:
+                osb[i] = work.tile([P, 4, S], F32, name="osb", bufs=3, align_bytes=64)
+            c = 1.0 / D**0.5
+            if eng == "s":
+                nc.scalar.activation(out=osb[i][:, 2 * h : 2 * h + 2, :], in_=ob[i, h][:], func=ACT.Copy, scale=c)
+            else:
+                nc.vector.tensor_scalar(out=osb[i][:, 2 * h : 2 * h + 2, :], in0=ob[i, h][:], scalar1=c, scalar2=None, op0=ALU.mult)
+            dst = orows[NT * i : NT * (i + 1), :].rearrange("(q j) s -> q j s", j=4)
+            if i == NB - 1:
+                nc.sync.dma_start(out=dst[:, 2 * h : 2 * h + 2, :], in_=osb[i][:, 2 * h : 2 * h + 2, :])
+            elif h == 1:
+                nc.sync.dma_start(out=dst, in_=osb[i][:])
+
+        def ktrans(b):
+            if not 0 <= b < B:
+                return
+            bank = psum.tile([P, 2, 2, P], F32, name="q", bufs=4)
+            kt[b] = bank
+            for h in range(2):
+                words = kb[b][:, h, :].bitcast(F32)
+                for u in range(2):
+                    nc.tensor.transpose(bank[:, h, u, :], words[:, u::2], ident[:])
+
+        def kcopy(b, eng="s"):
+            if not 0 <= b < B:
+                return
+            kg[b] = work.tile([P, 4 * S], BF16, name="kg", bufs=2, align_bytes=64)
+            (nc.scalar.copy if eng == "s" else nc.vector.tensor_copy)(
+                out=kg[b][:].bitcast(F32).rearrange("p (h q u) -> p h q u", h=2, u=2),
+                in_=kt[b][:].rearrange("p h u q -> p h q u"),
+            )
+
+        def kquant(b):
+            if not 0 <= b < B:
+                return
+            nc.vector.quantize_mx(out=k_codes[:, b, :].bitcast(FP8X4), scales=k_scales[:, b, :], in_=kg[b][:])
+
+        w_g = keep.tile([P, 4 * D], BF16, name="w_g", align_bytes=64)
+        wt = {}
+
+        def wtrans(h):
+            bank = psum.tile([P, 2, 2, P], F32, name="q", bufs=4)
+            wt[h] = bank
+            for tt in range(2):
+                words = w_raw[:, 2 * h + tt, :].bitcast(F32)
+                for u in range(2):
+                    nc.tensor.transpose(bank[:, tt, u, :], words[:, u::2], ident[:])
+
+        def wcopy(h, eng):
+            (nc.scalar.copy if eng == "s" else nc.vector.tensor_copy)(
+                out=w_g[:].bitcast(F32)[:, 512 * h : 512 * (h + 1)].rearrange("p (t m u) -> p t m u", t=2, u=2),
+                in_=wt[h][:].rearrange("p t u m -> p t m u"),
+            )
+
+        for j in range(4):
+            xp(0, j, j + 1)
+        nc.scalar.copy(out=scale[:, 1, :], in_=scale[:, 0, :])
+        nc.gpsimd.tensor_copy(out=bias[:], in_=b_raw[:])
+        nc.gpsimd.tensor_copy(out=gain[:], in_=g_raw[:])
+        nc.gpsimd.tensor_mul(out=bias_gain[:], in0=bias[:], in1=gain[:])
+        xt_half(0, 0)
+        wtrans(0)
+        xt_half(0, 1)
+        wtrans(1)
+        xcopy(0, 0, "s")
+        wcopy(0, "s")
+        xcopy(0, 1, "s")
+        wcopy(1, "v")
+        xquant(0)
+        nc.vector.quantize_mx(out=w_codes[:].bitcast(FP8X4), scales=w_scales[:], in_=w_g[:])
+        ktrans(0)
+        kcopy(0)
+        mm1(0, 0)
+        mm1(0, 1)
+        mm1(0, 2)
+        xp(1, 0, 2)
+        xt_half(1, 0)
+        xp(1, 2, 4)
+        xt_half(1, 1)
+        xp(2, 0, 2)
+        kquant(0)
+        xp(2, 2, 4)
+
+        for s in range(NB):
+            last = s == NB - 1
+            kn = s // 2 + 1
+            has_k = s % 2 == 0 and kn < B
+            normalise(s - 2)
+            sum_squares(s - 1, 0)
+            if s > 0:
+                mm1(s, 2)
+            if last:
+                mm1(s, 3)
+                for t in range(4):
+                    square(s, t)
+            else:
+                square_and_affine(s, 0)
+            sum_squares(s - 1, 1)
+            if not last:
+                square_and_affine(s, 1)
+            mm2(s - 3, 0)
+            if not last:
+                mm1(s, 3)
+            xcopy(s + 1, 0, "s")
+            xcopy(s + 1, 1, "s")
+            xp(s + 3, 0, 2)
+            mean_and_rstd(s - 1)
+            if last:
+                affine(s, 0)
+                affine(s, 1)
+                affine(s, 2)
+                affine(s, 3)
+            else:
+                square_and_affine(s, 2)
+            ocopy(s - 3, 0, "s")
+            if last:
+                spread_rstd(s - 1)
+                sum_squares(s, 0)
+            mm2(s - 3, 1)
+            if last:
+                sum_squares(s, 1)
+            xt_half(s + 2, 0)
+            xquant(s + 1)
+            xp(s + 3, 2, 4)
+            if has_k:
+                ktrans(kn)
+            mm1(s + 1, 0)
+            if not last:
+                square_and_affine(s, 3)
+            ocopy(s - 3, 1, "s" if s >= NB - 2 else "v")
+            if has_k:
+                kcopy(kn)
+            yquant(s - 2)
+            if has_k:
+                kquant(kn)
+            xt_half(s + 2, 1)
+            if not last and s < NB:
+                spread_rstd(s - 1)
+            mm1(s + 1, 1)
+
+        normalise(NB - 2)
+        mean_and_rstd(NB - 1)
+        yquant(NB - 2)
+        mm2(NB - 3, 0)
+        mm2(NB - 3, 1)
+        ocopy(NB - 3, 0, "s")
+        ocopy(NB - 3, 1, "s")
+        spread_rstd(NB - 1)
+        mm2(NB - 2, 0)
+        mm2(NB - 2, 1)
+        ocopy(NB - 2, 0, "s")
+        ocopy(NB - 2, 1, "s")
+        for h in range(2):
+            normalise(NB - 1, 256 * h, 256 * (h + 1))
+        for h in range(2):
+            yquant(NB - 1, 256 * h, 256 * (h + 1))
+            mm2(NB - 1, h)
+            ocopy(NB - 1, h, "s" if h == 0 else "v")

@@ -60,8 +60,6 @@ def tile_crossattention_pb_t_kernel(tc, text_bytes, text_scale, Wq_w, Wq_b, qn_w
 
         ident = keep.tile([P, P], F32, name="ident", align_bytes=64)
         make_identity(nc, ident[:])
-        ones = keep.tile([P, 1], F32, name="ones")
-        nc.gpsimd.memset(ones[:], 1.0)
         neg_half = keep.tile([P, 4], F32, name="neg_half")
         nc.gpsimd.memset(neg_half[:], -0.5)
         bias = keep.tile([P, 4], F32, name="bias")
@@ -172,13 +170,14 @@ def tile_crossattention_pb_t_kernel(tc, text_bytes, text_scale, Wq_w, Wq_b, qn_w
             if not 0 <= i < NB:
                 return
             if h == 0:
-                ssum[i] = psum.tile([P, 4], F32, name="s", bufs=1)
+                ssum[i] = psum.tile([P, 4, P], F32, name="s", bufs=1)
             for j in (2 * h, 2 * h + 1):
                 for t in range(4):
                     nc.tensor.matmul(
-                        out=ssum[i][:, j : j + 1],
+                        out=ssum[i][:, j, :],
                         lhsT=sq[i][:, t, P * j : P * (j + 1)],
-                        rhs=ones[:],
+                        rhs=ident[:],
+                        is_transpose=True,
                         start=(t == 0),
                         stop=(t == 3),
                     )
@@ -186,8 +185,10 @@ def tile_crossattention_pb_t_kernel(tc, text_bytes, text_scale, Wq_w, Wq_b, qn_w
         def mean_and_rstd(i):
             if not 0 <= i < NB:
                 return
+            tot = work.tile([P, 4], F32, name="tot", bufs=2)
+            nc.vector.tensor_reduce(out=tot[:], in_=ssum[i][:], axis=AX.X, op=ALU.add)
             ms = work.tile([P, 4], F32, name="ms", bufs=2)
-            nc.vector.tensor_scalar(out=ms[:], in0=ssum[i][:], scalar1=1.0 / D, scalar2=EPS, op0=ALU.mult, op1=ALU.add)
+            nc.gpsimd.tensor_scalar(out=ms[:], in0=tot[:], scalar1=1.0 / D, scalar2=EPS, op0=ALU.mult, op1=ALU.add)
             r = work.tile([P, 4], F32, name="rstd", bufs=2)
             nc.gpsimd.tensor_tensor(out=r[:], in0=ms[:], in1=neg_half[:], op=ALU.pow)
             rstd[i] = r
@@ -333,56 +334,50 @@ def tile_crossattention_pb_t_kernel(tc, text_bytes, text_scale, Wq_w, Wq_b, qn_w
             kn = s // 2 + 1
             has_k = s % 2 == 0 and kn < B
             normalise(s - 2)
+            xcopy(s + 1, 0, "s")
+            xcopy(s + 1, 1, "s")
             sum_squares(s - 1, 0)
             if s > 0:
                 mm1(s, 2)
+            sum_squares(s - 1, 1)
             if last:
                 mm1(s, 3)
                 for t in range(4):
                     square(s, t)
             else:
                 square_and_affine(s, 0)
-            sum_squares(s - 1, 1)
-            if not last:
                 square_and_affine(s, 1)
             mm2(s - 3, 0)
             if not last:
                 mm1(s, 3)
-            xcopy(s + 1, 0, "s")
-            xcopy(s + 1, 1, "s")
-            xp(s + 3, 0, 2)
+            xquant(s + 1)
             mean_and_rstd(s - 1)
+            xp(s + 3, 0, 2)
             if last:
-                affine(s, 0)
-                affine(s, 1)
-                affine(s, 2)
-                affine(s, 3)
+                for t in range(4):
+                    affine(s, t)
             else:
                 square_and_affine(s, 2)
             ocopy(s - 3, 0, "s")
             if last:
-                spread_rstd(s - 1)
                 sum_squares(s, 0)
             mm2(s - 3, 1)
             if last:
                 sum_squares(s, 1)
+            yquant(s - 2)
             xt_half(s + 2, 0)
-            xquant(s + 1)
             xp(s + 3, 2, 4)
             if has_k:
                 ktrans(kn)
             mm1(s + 1, 0)
             if not last:
                 square_and_affine(s, 3)
-            ocopy(s - 3, 1, "s" if s >= NB - 2 else "v")
+            ocopy(s - 3, 1, "v" if s % 2 == 1 and s < NB - 2 else "s")
             if has_k:
                 kcopy(kn)
-            yquant(s - 2)
-            if has_k:
                 kquant(kn)
             xt_half(s + 2, 1)
-            if not last and s < NB:
-                spread_rstd(s - 1)
+            spread_rstd(s - 1)
             mm1(s + 1, 1)
 
         normalise(NB - 2)

@@ -15,386 +15,395 @@ AX = mybir.AxisListType
 
 B, T, S, D = 8, 1024, 256, 512
 P = 128
-NT = 512
-NB = B * T // NT
+PACK = 4
+NTOK = 512
+NJ = NTOK // P
+HALF = NTOK // 2
+NB = B * T // NTOK
+PER_B = T // NTOK
+WORDS = D // 2
+GROUP = 4
 EPS = 1e-6
 FLOPS = 2 * B * T * D * D + 2 * B * T * S * D
 
 
 def tile_crossattention_pb_t_kernel(tc, text_bytes, text_scale, Wq_w, Wq_b, qn_w, k_norm, out):
     nc = tc.nc
-    xrows = text_bytes.rearrange("b t k -> (b t) k")
-    orows = out.rearrange("b t s -> (b t) s")
+    text_rows = text_bytes.rearrange("b t k -> (b t) k")
+    out_rows = out.rearrange("b t s -> (b t) s")
 
     with ExitStack() as ctx:
         keep = ctx.enter_context(tc.tile_pool(name="keep", bufs=1))
-        raw = ctx.enter_context(tc.tile_pool(name="raw", bufs=1))
         work = ctx.enter_context(tc.tile_pool(name="work", bufs=2))
         psum = ctx.enter_context(tc.psum_pool(name="psum", bufs=1))
         ctx.enter_context(tc.manual_schedule())
 
-        xb = {}
-        kb = {}
+        scale_cols = keep.tile([P, PACK], F32, name="scale_cols")
+        nc.scalar.dma_start(out=scale_cols[:], in_=text_scale.rearrange("a b (p t) -> (a b p) t", t=PACK))
+        bias = keep.tile([P, PACK], BF16, name="bias")
+        nc.scalar.dma_start(out=bias[:], in_=Wq_b.rearrange("(p t) -> p t", t=PACK))
+        gain_bf16 = keep.tile([P, PACK], BF16, name="gain_bf16")
+        nc.scalar.dma_start(out=gain_bf16[:], in_=qn_w.rearrange("(p t) -> p t", t=PACK))
+        wq = keep.tile([P, PACK, D], BF16, name="wq", align_bytes=64)
+        nc.sync.dma_start(out=wq[:], in_=Wq_w.rearrange("(m t) k -> m t k", t=PACK))
 
-        def load_x(i):
-            xb[i] = raw.tile([P, 4, D], U8, name="xbytes", bufs=NB, align_bytes=64)
-            nc.sync.dma_start(out=xb[i][:], in_=xrows[NT * i : NT * (i + 1), :].rearrange("(q j) k -> q j k", j=4))
+        byte_tiles = []
+        keys = []
+        for i in range(NB):
+            byte_tile = keep.tile([P, NJ, D], U8, name="byte_tile", bufs=NB, align_bytes=64)
+            rows = text_rows[NTOK * i : NTOK * (i + 1), :]
+            nc.sync.dma_start(out=byte_tile[:], in_=rows.rearrange("(r j) k -> r j k", j=NJ))
+            byte_tiles.append(byte_tile)
+            if 1 <= i <= B:
+                keys_tile = keep.tile([P, 2, D], BF16, name="keys_tile", bufs=B, align_bytes=64)
+                nc.sync.dma_start(out=keys_tile[:], in_=k_norm[i - 1].rearrange("(h r) k -> r h k", r=P))
+                keys.append(keys_tile)
 
-        def load_k(b):
-            kb[b] = raw.tile([P, 2, D], BF16, name="kraw", bufs=B, align_bytes=64)
-            nc.sync.dma_start(out=kb[b][:], in_=k_norm[b].rearrange("(h q) k -> q h k", q=P))
-
-        scale = keep.tile([P, 2, D], F32, name="scale", align_bytes=64)
-        nc.scalar.dma_start(out=scale[:, 0, :], in_=text_scale.rearrange("a b k -> (a b k)").partition_broadcast(P))
-        load_x(0)
-        b_raw = keep.tile([P, 4], BF16, name="b_raw")
-        nc.scalar.dma_start(out=b_raw[:], in_=Wq_b.rearrange("(p t) -> p t", t=4))
-        g_raw = keep.tile([P, 4], BF16, name="g_raw")
-        nc.scalar.dma_start(out=g_raw[:], in_=qn_w.rearrange("(p t) -> p t", t=4))
-        w_raw = keep.tile([P, 4, D], BF16, name="w_raw", align_bytes=64)
-        nc.sync.dma_start(out=w_raw[:], in_=Wq_w.rearrange("(m t) k -> m t k", t=4))
-        for i in range(1, NB):
-            load_x(i)
-            if i <= B:
-                load_k(i - 1)
-
+        zeros = keep.tile([P, NTOK], BF16, name="zeros", align_bytes=64)
+        nc.vector.memset(zeros[:], 0.0)
         ident = keep.tile([P, P], F32, name="ident", align_bytes=64)
         make_identity(nc, ident[:])
-        neg_half = keep.tile([P, 4], F32, name="neg_half")
-        nc.gpsimd.memset(neg_half[:], -0.5)
-        bias = keep.tile([P, 4], F32, name="bias")
-        gain = keep.tile([P, 4], F32, name="gain")
-        bias_gain = keep.tile([P, 4], F32, name="bias_gain")
+        eps = keep.tile([P, 1], F32, name="eps")
+        nc.gpsimd.memset(eps[:], EPS)
+        text_scales = keep.tile([P, 2, D], F32, name="text_scales", align_bytes=64)
+        gain = keep.tile([P, PACK], F32, name="gain")
+        bias_gain = keep.tile([P, PACK], F32, name="bias_gain")
 
-        w_codes = keep.tile([P, D], U32, name="w_codes", align_bytes=64)
-        w_scales = keep.tile([P, D], U8, name="w_scales", align_bytes=64)
-        k_codes = keep.tile([P, B, S], U32, name="k_codes", align_bytes=64)
-        k_scales = keep.tile([P, B, S], U8, name="k_scales", align_bytes=64)
+        wq_pairs = keep.tile([P, PACK * D], BF16, name="wq_pairs", align_bytes=64)
+        wq_codes = keep.tile([P, D], U32, name="wq_codes", align_bytes=64)
+        wq_scales = keep.tile([P, D], U8, name="wq_scales", align_bytes=64)
+        key_codes = keep.tile([P, B, S], U32, name="key_codes", align_bytes=64)
+        key_scales = keep.tile([P, B, S], U8, name="key_scales", align_bytes=64)
 
-        xs = {}
-        xt = {}
-        xg = {}
-        xc = {}
-        q = {}
-        sq = {}
-        z = {}
-        ssum = {}
-        rstd = {}
-        rb = {}
-        y = {}
-        yc = {}
-        ob = {}
-        osb = {}
-        kt = {}
-        kg = {}
+        text_bf16, text_turned, text_pairs, text_mx = {}, {}, {}, {}
+        q_banks, squares, affine_q = {}, {}, {}
+        square_sums, rstd, rstd_spread = {}, {}, {}
+        y_pairs, y_mx, score_banks, scores = {}, {}, {}, {}
+        wq_turned, key_turned, key_pairs = {}, {}, {}
 
-        def xp(i, lo, hi):
-            if not 0 <= i < NB:
-                return
-            if lo == 0:
-                xs[i] = work.tile([P, 4 * D], BF16, name="xs", bufs=4, align_bytes=64)
-            bytes_flat = xb[i][:].rearrange("p j k -> p (j k)")
-            scale_flat = scale[:].rearrange("p j k -> p (j k)")
-            nc.vector.tensor_tensor(
-                out=xs[i][:, D * lo : D * hi],
-                in0=bytes_flat[:, D * lo : D * hi].bitcast(FP8),
-                in1=scale_flat[:, 0 : D * (hi - lo)],
-                op=ALU.mult,
-            )
+        def main_bank(shape):
+            bank = psum.tile(shape, F32, name="main", bufs=4)
+            return bank
 
-        def xt_half(i, h):
-            if not 0 <= i < NB:
-                return
-            bank = psum.tile([P, 2, 2, P], F32, name="xt", bufs=2)
-            xt[i, h] = bank
-            words = xs[i][:].bitcast(F32)
-            for jj in range(2):
-                j = 2 * h + jj
+        def keep_clock(bank, count=1):
+            for n in range(count):
+                nc.tensor.matmul(out=bank, lhsT=zeros[:, 0:P], rhs=zeros[:], start=True, stop=True)
+
+        def turn_two_row_tiles(bank, row_tiles):
+            for n, rows in enumerate(row_tiles):
+                words = rows.bitcast(F32)
                 for u in range(2):
-                    nc.tensor.transpose(bank[:, jj, u, :], words[:, 256 * j + u : 256 * (j + 1) : 2], ident[:])
+                    nc.tensor.transpose(bank[:, n, u, :], words[:, u:WORDS:2], ident[:])
 
-        def xcopy(i, h, eng):
+        def copy_pairs(copy, pairs, part, bank):
+            dst = pairs[:].bitcast(F32)[:, 4 * P * part : 4 * P * (part + 1)]
+            copy(out=dst.rearrange("p (n r u) -> p n r u", n=2, u=2), in_=bank[:].rearrange("p n u r -> p n r u"))
+
+        def turn_wq(part):
+            wq_turned[part] = main_bank([P, 2, 2, P])
+            turn_two_row_tiles(wq_turned[part], [wq[:, 2 * part + n, :] for n in range(2)])
+
+        def turn_keys(b):
+            key_turned[b] = main_bank([P, 2, 2, P])
+            turn_two_row_tiles(key_turned[b], [keys[b][:, h, :] for h in range(2)])
+
+        def copy_keys(b):
+            key_pairs[b] = work.tile([P, PACK * S], BF16, name="key_pairs", align_bytes=64)
+            copy_pairs(nc.scalar.copy, key_pairs[b], 0, key_turned[b])
+
+        def quantise_keys(b):
+            nc.vector.quantize_mx(out=key_codes[:, b, :].bitcast(FP8X4), scales=key_scales[:, b, :], in_=key_pairs[b][:])
+
+        def scale_text(i, half, parts=1):
             if not 0 <= i < NB:
                 return
-            if h == 0:
-                xg[i] = work.tile([P, 4 * NT], BF16, name="xg", bufs=3, align_bytes=64)
-            dst = xg[i][:].bitcast(F32)[:, 512 * h : 512 * (h + 1)].rearrange("p (j q u) -> p j q u", j=2, u=2)
-            src = xt[i, h][:].rearrange("p j u q -> p j q u")
-            if eng == "s":
-                nc.scalar.copy(out=dst, in_=src)
-            else:
-                nc.vector.tensor_copy(out=dst, in_=src)
+            if half == 0:
+                text_bf16[i] = work.tile([P, NJ * D], BF16, name="text_bf16", bufs=4, align_bytes=64)
+            flat_bytes = byte_tiles[i][:].rearrange("r j k -> r (j k)")
+            flat_scales = text_scales[:].rearrange("r n k -> r (n k)")
+            width = 2 * D // parts
+            for part in range(parts):
+                cols = slice(2 * D * half + width * part, 2 * D * half + width * (part + 1))
+                nc.vector.tensor_tensor(
+                    out=text_bf16[i][:, cols], in0=flat_bytes[:, cols].bitcast(FP8), in1=flat_scales[:, 0:width], op=ALU.mult
+                )
 
-        def xquant(i):
+        def turn_text(i, half, fill=True):
             if not 0 <= i < NB:
                 return
-            codes = work.tile([P, NT], U32, name="xcodes", bufs=3, align_bytes=64)
-            scl = work.tile([P, NT], U8, name="xscales", bufs=3, align_bytes=64)
-            xc[i] = (codes, scl)
-            nc.vector.quantize_mx(out=codes[:].bitcast(FP8X4), scales=scl[:], in_=xg[i][:])
+            bank = psum.tile([P, 2, 2, P], F32, name="text_bank", bufs=2)
+            text_turned[i, half] = bank
+            if fill:
+                keep_clock(bank[:].rearrange("p n u r -> p (n u r)"))
+            turn_two_row_tiles(bank, [text_bf16[i][:, D * j : D * (j + 1)] for j in (2 * half, 2 * half + 1)])
 
-        def mm1(i, t):
+        def copy_text(i, half):
             if not 0 <= i < NB:
                 return
-            bank = psum.tile([P, NT], F32, name="q", bufs=4)
-            q[i, t] = bank
-            codes, scl = xc[i]
+            if half == 0:
+                text_pairs[i] = work.tile([P, PACK * NTOK], BF16, name="text_pairs", bufs=3, align_bytes=64)
+            copy_pairs(nc.scalar.copy, text_pairs[i], half, text_turned[i, half])
+
+        def quantise_text(i):
+            if not 0 <= i < NB:
+                return
+            codes = work.tile([P, NTOK], U32, name="text_codes", bufs=3, align_bytes=64)
+            scales = work.tile([P, NTOK], U8, name="text_mx_scales", bufs=3, align_bytes=64)
+            nc.vector.quantize_mx(out=codes[:].bitcast(FP8X4), scales=scales[:], in_=text_pairs[i][:])
+            text_mx[i] = (codes, scales)
+
+        def project(i, t):
+            if not 0 <= i < NB:
+                return
+            q_banks[i, t] = main_bank([P, NTOK])
+            codes, scales = text_mx[i]
+            cols = slice(P * t, P * (t + 1))
             nc.tensor.matmul_mx(
-                out=bank[:],
-                lhsT=w_codes[:, P * t : P * (t + 1)].bitcast(FP8X4),
-                lhsT_scale=w_scales[:, P * t : P * (t + 1)],
+                out=q_banks[i, t][:],
+                lhsT=wq_codes[:, cols].bitcast(FP8X4),
+                lhsT_scale=wq_scales[:, cols],
                 rhs=codes[:].bitcast(FP8X4),
-                rhs_scale=scl[:],
+                rhs_scale=scales[:],
                 start=True,
                 stop=True,
             )
 
         def square(i, t):
-            if not 0 <= i < NB:
-                return
             if t == 0:
-                sq[i] = work.tile([P, 4, NT], F32, name="sq", bufs=2, align_bytes=64)
-                z[i] = work.tile([P, 4, NT], F32, name="z", bufs=3, align_bytes=64)
-            nc.scalar.activation(out=sq[i][:, t, :], in_=q[i, t][:], func=ACT.Square, bias=bias[:, t : t + 1], scale=1.0)
+                squares[i] = work.tile([P, PACK, NTOK], F32, name="squares", align_bytes=64)
+                affine_q[i] = work.tile([P, PACK, NTOK], F32, name="affine_q", bufs=3, align_bytes=64)
+            nc.scalar.activation(out=squares[i][:, t, :], in_=q_banks[i, t][:], func=ACT.Square, bias=bias[:, t : t + 1])
 
-        def affine(i, t):
-            if not 0 <= i < NB:
-                return
-            nc.scalar.activation(out=z[i][:, t, :], in_=q[i, t][:], func=ACT.Identity, bias=bias_gain[:, t : t + 1], scale=gain[:, t : t + 1])
+        def apply_gain(i, t):
+            nc.scalar.activation(
+                out=affine_q[i][:, t, :],
+                in_=q_banks[i, t][:],
+                func=ACT.Identity,
+                bias=bias_gain[:, t : t + 1],
+                scale=gain[:, t : t + 1],
+            )
 
-        def square_and_affine(i, t):
+        def square_and_gain(i, t):
             square(i, t)
-            affine(i, t)
+            apply_gain(i, t)
 
-        def sum_squares(i, h):
+        def sum_slices(i):
             if not 0 <= i < NB:
                 return
-            if h == 0:
-                ssum[i] = psum.tile([P, 4, P], F32, name="s", bufs=1)
-            for j in (2 * h, 2 * h + 1):
-                for t in range(4):
+            square_sums[i] = psum.tile([P, NJ, P], F32, name="sum_bank")
+            for j in range(NJ):
+                for t in range(PACK):
                     nc.tensor.matmul(
-                        out=ssum[i][:, j, :],
-                        lhsT=sq[i][:, t, P * j : P * (j + 1)],
+                        out=square_sums[i][:, j, :],
+                        lhsT=squares[i][:, t, P * j : P * (j + 1)],
                         rhs=ident[:],
                         is_transpose=True,
                         start=(t == 0),
-                        stop=(t == 3),
+                        stop=(t == PACK - 1),
                     )
 
-        def mean_and_rstd(i):
+        def sum_features(i, parts=1):
             if not 0 <= i < NB:
                 return
-            tot = work.tile([P, 4], F32, name="tot", bufs=2)
-            nc.vector.tensor_reduce(out=tot[:], in_=ssum[i][:], axis=AX.X, op=ALU.add)
-            ms = work.tile([P, 4], F32, name="ms", bufs=2)
-            nc.gpsimd.tensor_scalar(out=ms[:], in0=tot[:], scalar1=1.0 / D, scalar2=EPS, op0=ALU.mult, op1=ALU.add)
-            r = work.tile([P, 4], F32, name="rstd", bufs=2)
-            nc.gpsimd.tensor_tensor(out=r[:], in0=ms[:], in1=neg_half[:], op=ALU.pow)
-            rstd[i] = r
+            rstd[i] = []
+            n = NJ // parts
+            for part in range(parts):
+                total = work.tile([P, NJ], F32, name="total", bufs=4)
+                nc.vector.tensor_reduce(
+                    out=total[:, 0:n], in_=square_sums[i][:, n * part : n * (part + 1), :], axis=AX.X, op=ALU.add
+                )
+                root = work.tile([P, NJ], F32, name="root", bufs=4)
+                rstd[i].append((total, root))
 
-        def spread_rstd(i):
+        def take_roots(i):
             if not 0 <= i < NB:
                 return
-            bank = psum.tile([P, NT], F32, name="r", bufs=1)
-            rb[i] = bank
-            for j in range(4):
-                nc.tensor.transpose(bank[:, P * j : P * (j + 1)], rstd[i][:, j : j + 1].to_broadcast([P, P]), ident[:])
+            n = NJ // len(rstd[i])
+            for total, root in rstd[i]:
+                nc.scalar.activation(
+                    out=root[:, 0:n], in_=total[:, 0:n], func=ACT.Abs_reciprocal_sqrt, scale=1.0 / D, bias=eps[:, 0:1]
+                )
 
-        def normalise(i, lo=0, hi=NT):
+        def spread_roots(i):
+            if not 0 <= i < NB:
+                return
+            rstd_spread[i] = psum.tile([P, NTOK], F32, name="root_bank")
+            n = NJ // len(rstd[i])
+            for j in range(NJ):
+                root = rstd[i][j // n][1]
+                column = root[:, j % n : j % n + 1]
+                nc.tensor.transpose(rstd_spread[i][:, P * j : P * (j + 1)], column.to_broadcast([P, P]), ident[:])
+
+        def normalise(i, lo=0, hi=NTOK):
             if not 0 <= i < NB:
                 return
             if lo == 0:
-                y[i] = work.tile([P, 4 * NT], BF16, name="y", bufs=2, align_bytes=64)
-            n = hi - lo
+                y_pairs[i] = work.tile([P, PACK * NTOK], BF16, name="y_pairs", align_bytes=64)
+            roots = rstd_spread[i][:, lo:hi].rearrange("p (c n) -> p c n", n=GROUP).unsqueeze(2)
             nc.vector.tensor_tensor(
-                out=y[i][:, 4 * lo : 4 * hi].rearrange("p (c i t) -> p c t i", i=4, t=4),
-                in0=z[i][:, :, lo:hi].rearrange("p t (c i) -> p c t i", i=4),
-                in1=rb[i][:, lo:hi].rearrange("p (c i) -> p c i", i=4).unsqueeze(2).to_broadcast([P, n // 4, 4, 4]),
+                out=y_pairs[i][:, PACK * lo : PACK * hi].rearrange("p (c n t) -> p c t n", n=GROUP, t=PACK),
+                in0=affine_q[i][:, :, lo:hi].rearrange("p t (c n) -> p c t n", n=GROUP),
+                in1=roots.to_broadcast([P, (hi - lo) // GROUP, PACK, GROUP]),
                 op=ALU.mult,
             )
 
-        def yquant(i, lo=0, hi=NT):
+        def quantise_y(i, lo=0, hi=NTOK):
             if not 0 <= i < NB:
                 return
             if lo == 0:
-                codes = work.tile([P, NT], U32, name="ycodes", bufs=2, align_bytes=64)
-                scl = work.tile([P, NT], U8, name="yscales", bufs=2, align_bytes=64)
-                yc[i] = (codes, scl)
-            codes, scl = yc[i]
-            nc.vector.quantize_mx(out=codes[:, lo:hi].bitcast(FP8X4), scales=scl[:, lo:hi], in_=y[i][:, 4 * lo : 4 * hi])
+                codes = work.tile([P, NTOK], U32, name="y_codes", align_bytes=64)
+                scales = work.tile([P, NTOK], U8, name="y_scales", align_bytes=64)
+                y_mx[i] = (codes, scales)
+            codes, scales = y_mx[i]
+            nc.vector.quantize_mx(
+                out=codes[:, lo:hi].bitcast(FP8X4), scales=scales[:, lo:hi], in_=y_pairs[i][:, PACK * lo : PACK * hi]
+            )
 
-        def mm2(i, h):
+        def score(i, half):
             if not 0 <= i < NB:
                 return
-            b = i // 2
-            codes, scl = yc[i]
-            bank = psum.tile([P, 2, S], F32, name="q", bufs=4)
-            ob[i, h] = bank
-            for jj in range(2):
-                cols = slice(P * (2 * h + jj), P * (2 * h + jj + 1))
+            b = i // PER_B
+            codes, scales = y_mx[i]
+            bank = main_bank([P, 2, S])
+            score_banks[i, half] = bank
+            for n in range(2):
+                cols = slice(P * (2 * half + n), P * (2 * half + n + 1))
                 nc.tensor.matmul_mx(
-                    out=bank[:, jj, :],
+                    out=bank[:, n, :],
                     lhsT=codes[:, cols].bitcast(FP8X4),
-                    lhsT_scale=scl[:, cols],
-                    rhs=k_codes[:, b, :].bitcast(FP8X4),
-                    rhs_scale=k_scales[:, b, :],
+                    lhsT_scale=scales[:, cols],
+                    rhs=key_codes[:, b, :].bitcast(FP8X4),
+                    rhs_scale=key_scales[:, b, :],
                     start=True,
                     stop=True,
                 )
 
-        def ocopy(i, h, eng):
+        def store(i, half, on_vector=False):
             if not 0 <= i < NB:
                 return
-            if h == 0:
-                osb[i] = work.tile([P, 4, S], F32, name="osb", bufs=3, align_bytes=64)
-            c = 1.0 / D**0.5
-            if eng == "s":
-                nc.scalar.activation(out=osb[i][:, 2 * h : 2 * h + 2, :], in_=ob[i, h][:], func=ACT.Copy, scale=c)
+            if half == 0:
+                scores[i] = work.tile([P, NJ, S], F32, name="scores", bufs=3, align_bytes=64)
+            part = scores[i][:, 2 * half : 2 * half + 2, :]
+            factor = 1.0 / D**0.5
+            if on_vector:
+                nc.vector.tensor_scalar(out=part, in0=score_banks[i, half][:], scalar1=factor, scalar2=None, op0=ALU.mult)
             else:
-                nc.vector.tensor_scalar(out=osb[i][:, 2 * h : 2 * h + 2, :], in0=ob[i, h][:], scalar1=c, scalar2=None, op0=ALU.mult)
-            dst = orows[NT * i : NT * (i + 1), :].rearrange("(q j) s -> q j s", j=4)
+                nc.scalar.activation(out=part, in_=score_banks[i, half][:], func=ACT.Copy, scale=factor)
+            dst = out_rows[NTOK * i : NTOK * (i + 1), :].rearrange("(r j) s -> r j s", j=NJ)
             if i == NB - 1:
-                nc.sync.dma_start(out=dst[:, 2 * h : 2 * h + 2, :], in_=osb[i][:, 2 * h : 2 * h + 2, :])
-            elif h == 1:
-                nc.sync.dma_start(out=dst, in_=osb[i][:])
+                nc.sync.dma_start(out=dst[:, 2 * half : 2 * half + 2, :], in_=part)
+            elif half == 1:
+                nc.sync.dma_start(out=dst, in_=scores[i][:])
 
-        def ktrans(b):
-            if not 0 <= b < B:
-                return
-            bank = psum.tile([P, 2, 2, P], F32, name="q", bufs=4)
-            kt[b] = bank
-            for h in range(2):
-                words = kb[b][:, h, :].bitcast(F32)
-                for u in range(2):
-                    nc.tensor.transpose(bank[:, h, u, :], words[:, u::2], ident[:])
+        idle_bank = psum.tile([P, NTOK], F32, name="root_bank")
+        keep_clock(idle_bank[:], count=4)
+        scale_bank = psum.tile([P, PACK, P], F32, name="sum_bank")
+        for t in range(PACK):
+            nc.tensor.transpose(scale_bank[:, t, :], scale_cols[:, t : t + 1].to_broadcast([P, P]), ident[:])
+        for part, copy in enumerate((nc.scalar.copy, nc.vector.tensor_copy)):
+            dst = text_scales[:, part, :].rearrange("p (n t) -> p n t", t=PACK)
+            copy(out=dst, in_=scale_bank[:].rearrange("p t n -> p n t"))
+        turn_wq(0)
+        turn_wq(1)
+        copy_pairs(nc.scalar.copy, wq_pairs, 0, wq_turned[0])
+        copy_pairs(nc.scalar.copy, wq_pairs, 1, wq_turned[1])
+        scale_text(0, 0, parts=2)
+        scale_text(0, 1, parts=2)
+        scale_text(1, 0)
+        turn_text(0, 0, fill=False)
+        turn_text(0, 1, fill=False)
+        nc.vector.quantize_mx(out=wq_codes[:].bitcast(FP8X4), scales=wq_scales[:], in_=wq_pairs[:])
+        nc.vector.tensor_copy(out=gain[:], in_=gain_bf16[:])
+        nc.vector.tensor_mul(out=bias_gain[:], in0=bias[:], in1=gain_bf16[:])
+        copy_text(0, 0)
+        copy_text(0, 1)
+        quantise_text(0)
+        turn_text(1, 0, fill=False)
+        project(0, 0)
+        project(0, 1)
+        idle_bank = psum.tile([P, NTOK], F32, name="sum_bank")
+        keep_clock(idle_bank[:], count=4)
+        project(0, 2)
+        scale_text(1, 1)
+        turn_text(1, 1, fill=False)
+        scale_text(2, 0)
+        scale_text(2, 1)
 
-        def kcopy(b, eng="s"):
-            if not 0 <= b < B:
-                return
-            kg[b] = work.tile([P, 4 * S], BF16, name="kg", bufs=2, align_bytes=64)
-            (nc.scalar.copy if eng == "s" else nc.vector.tensor_copy)(
-                out=kg[b][:].bitcast(F32).rearrange("p (h q u) -> p h q u", h=2, u=2),
-                in_=kt[b][:].rearrange("p h u q -> p h q u"),
-            )
-
-        def kquant(b):
-            if not 0 <= b < B:
-                return
-            nc.vector.quantize_mx(out=k_codes[:, b, :].bitcast(FP8X4), scales=k_scales[:, b, :], in_=kg[b][:])
-
-        w_g = keep.tile([P, 4 * D], BF16, name="w_g", align_bytes=64)
-        wt = {}
-
-        def wtrans(h):
-            bank = psum.tile([P, 2, 2, P], F32, name="q", bufs=4)
-            wt[h] = bank
-            for tt in range(2):
-                words = w_raw[:, 2 * h + tt, :].bitcast(F32)
-                for u in range(2):
-                    nc.tensor.transpose(bank[:, tt, u, :], words[:, u::2], ident[:])
-
-        def wcopy(h, eng):
-            (nc.scalar.copy if eng == "s" else nc.vector.tensor_copy)(
-                out=w_g[:].bitcast(F32)[:, 512 * h : 512 * (h + 1)].rearrange("p (t m u) -> p t m u", t=2, u=2),
-                in_=wt[h][:].rearrange("p t u m -> p t m u"),
-            )
-
-        for j in range(4):
-            xp(0, j, j + 1)
-        nc.scalar.copy(out=scale[:, 1, :], in_=scale[:, 0, :])
-        nc.gpsimd.tensor_copy(out=bias[:], in_=b_raw[:])
-        nc.gpsimd.tensor_copy(out=gain[:], in_=g_raw[:])
-        nc.gpsimd.tensor_mul(out=bias_gain[:], in0=bias[:], in1=gain[:])
-        xt_half(0, 0)
-        wtrans(0)
-        xt_half(0, 1)
-        wtrans(1)
-        xcopy(0, 0, "s")
-        wcopy(0, "s")
-        xcopy(0, 1, "s")
-        wcopy(1, "v")
-        xquant(0)
-        nc.vector.quantize_mx(out=w_codes[:].bitcast(FP8X4), scales=w_scales[:], in_=w_g[:])
-        ktrans(0)
-        kcopy(0)
-        mm1(0, 0)
-        mm1(0, 1)
-        mm1(0, 2)
-        xp(1, 0, 2)
-        xt_half(1, 0)
-        xp(1, 2, 4)
-        xt_half(1, 1)
-        xp(2, 0, 2)
-        kquant(0)
-        xp(2, 2, 4)
-
-        for s in range(NB):
-            last = s == NB - 1
-            kn = s // 2 + 1
-            has_k = s % 2 == 0 and kn < B
+        for s in range(NB - 1):
+            new_b = s % PER_B == 0
+            copy_text(s + 1, 0)
             normalise(s - 2)
-            xcopy(s + 1, 0, "s")
-            xcopy(s + 1, 1, "s")
-            sum_squares(s - 1, 0)
             if s > 0:
-                mm1(s, 2)
-            sum_squares(s - 1, 1)
-            if last:
-                mm1(s, 3)
-                for t in range(4):
-                    square(s, t)
-            else:
-                square_and_affine(s, 0)
-                square_and_affine(s, 1)
-            mm2(s - 3, 0)
-            if not last:
-                mm1(s, 3)
-            xquant(s + 1)
-            mean_and_rstd(s - 1)
-            xp(s + 3, 0, 2)
-            if last:
-                for t in range(4):
-                    affine(s, t)
-            else:
-                square_and_affine(s, 2)
-            ocopy(s - 3, 0, "s")
-            if last:
-                sum_squares(s, 0)
-            mm2(s - 3, 1)
-            if last:
-                sum_squares(s, 1)
-            yquant(s - 2)
-            xt_half(s + 2, 0)
-            xp(s + 3, 2, 4)
-            if has_k:
-                ktrans(kn)
-            mm1(s + 1, 0)
-            if not last:
-                square_and_affine(s, 3)
-            ocopy(s - 3, 1, "v" if s % 2 == 1 and s < NB - 2 else "s")
-            if has_k:
-                kcopy(kn)
-                kquant(kn)
-            xt_half(s + 2, 1)
-            spread_rstd(s - 1)
-            mm1(s + 1, 1)
+                project(s, 2)
+            sum_slices(s - 1)
+            score(s - 3, 0)
+            sum_features(s - 1)
+            square_and_gain(s, 0)
+            square_and_gain(s, 1)
+            turn_text(s + 2, 0)
+            scale_text(s + 3, 0)
+            copy_text(s + 1, 1)
+            if new_b:
+                turn_keys(s // PER_B)
+            quantise_text(s + 1)
+            square_and_gain(s, 2)
+            score(s - 3, 1)
+            take_roots(s - 1)
+            if new_b:
+                copy_keys(s // PER_B)
+            project(s, 3)
+            store(s - 3, 0)
+            turn_text(s + 2, 1)
+            spread_roots(s - 1)
+            store(s - 3, 1, on_vector=not new_b)
+            project(s + 1, 0)
+            square_and_gain(s, 3)
+            scale_text(s + 3, 1)
+            quantise_y(s - 2)
+            project(s + 1, 1)
+            if new_b:
+                quantise_keys(s // PER_B)
 
-        normalise(NB - 2)
-        mean_and_rstd(NB - 1)
-        yquant(NB - 2)
-        mm2(NB - 3, 0)
-        mm2(NB - 3, 1)
-        ocopy(NB - 3, 0, "s")
-        ocopy(NB - 3, 1, "s")
-        spread_rstd(NB - 1)
-        mm2(NB - 2, 0)
-        mm2(NB - 2, 1)
-        ocopy(NB - 2, 0, "s")
-        ocopy(NB - 2, 1, "s")
-        for h in range(2):
-            normalise(NB - 1, 256 * h, 256 * (h + 1))
-        for h in range(2):
-            yquant(NB - 1, 256 * h, 256 * (h + 1))
-            mm2(NB - 1, h)
-            ocopy(NB - 1, h, "s" if h == 0 else "v")
+        s = NB - 1
+        project(s, 2)
+        project(s, 3)
+        square(s, 0)
+        square(s, 1)
+        sum_slices(s - 1)
+        normalise(s - 2)
+        sum_features(s - 1)
+        apply_gain(s, 0)
+        apply_gain(s, 1)
+        square(s, 2)
+        square(s, 3)
+        take_roots(s - 1)
+        apply_gain(s, 2)
+        apply_gain(s, 3)
+        score(s - 3, 0)
+        score(s - 3, 1)
+        quantise_y(s - 2)
+        sum_slices(s)
+        spread_roots(s - 1)
+        sum_features(s, parts=2)
+        take_roots(s)
+        store(s - 3, 0)
+        store(s - 3, 1)
+        normalise(s - 1)
+        score(s - 2, 0)
+        score(s - 2, 1)
+        store(s - 2, 0)
+        store(s - 2, 1)
+        spread_roots(s)
+        quantise_y(s - 1)
+        normalise(s, 0, HALF)
+        normalise(s, HALF, NTOK)
+        score(s - 1, 0)
+        score(s - 1, 1)
+        store(s - 1, 0)
+        store(s - 1, 1)
+        quantise_y(s, 0, HALF)
+        score(s, 0)
+        store(s, 0)
+        quantise_y(s, HALF, NTOK)
+        score(s, 1)
+        store(s, 1, on_vector=True)

from contextlib import ExitStack

import concourse.mybir as mybir
from concourse.masks import make_identity

F32 = mybir.dt.float32
BF16 = mybir.dt.bfloat16
U32 = mybir.dt.uint32
U8 = mybir.dt.uint8
FP8 = mybir.dt.float8_e4m3fn
FP8X4 = mybir.dt.float8_e4m3fn_x4
ACT = mybir.ActivationFunctionType
ALU = mybir.AluOpType
AX = mybir.AxisListType

B, T, S, D = 8, 1024, 256, 512
P = 128
PACK = 4
NTOK = 512
NJ = NTOK // P
HALF = NTOK // 2
NB = B * T // NTOK
PER_B = T // NTOK
WORDS = D // 2
GROUP = 4
EPS = 1e-6
FLOPS = 2 * B * T * D * D + 2 * B * T * S * D


def tile_crossattention_pb_t_kernel(tc, text_bytes, text_scale, Wq_w, Wq_b, qn_w, k_norm, out):
    nc = tc.nc
    text_rows = text_bytes.rearrange("b t k -> (b t) k")
    out_rows = out.rearrange("b t s -> (b t) s")

    with ExitStack() as ctx:
        keep = ctx.enter_context(tc.tile_pool(name="keep", bufs=1))
        work = ctx.enter_context(tc.tile_pool(name="work", bufs=2))
        psum = ctx.enter_context(tc.psum_pool(name="psum", bufs=1))
        ctx.enter_context(tc.manual_schedule())

        scale_cols = keep.tile([P, PACK], F32, name="scale_cols")
        nc.scalar.dma_start(out=scale_cols[:], in_=text_scale.rearrange("a b (p t) -> (a b p) t", t=PACK))
        bias = keep.tile([P, PACK], BF16, name="bias")
        nc.scalar.dma_start(out=bias[:], in_=Wq_b.rearrange("(p t) -> p t", t=PACK))
        gain_bf16 = keep.tile([P, PACK], BF16, name="gain_bf16")
        nc.scalar.dma_start(out=gain_bf16[:], in_=qn_w.rearrange("(p t) -> p t", t=PACK))
        wq = keep.tile([P, PACK, D], BF16, name="wq", align_bytes=64)
        nc.sync.dma_start(out=wq[:], in_=Wq_w.rearrange("(m t) k -> m t k", t=PACK))

        byte_tiles = []
        keys = []
        for i in range(NB):
            byte_tile = keep.tile([P, NJ, D], U8, name="byte_tile", bufs=NB, align_bytes=64)
            rows = text_rows[NTOK * i : NTOK * (i + 1), :]
            nc.sync.dma_start(out=byte_tile[:], in_=rows.rearrange("(r j) k -> r j k", j=NJ))
            byte_tiles.append(byte_tile)
            if 1 <= i <= B:
                keys_tile = keep.tile([P, 2, D], BF16, name="keys_tile", bufs=B, align_bytes=64)
                nc.sync.dma_start(out=keys_tile[:], in_=k_norm[i - 1].rearrange("(h r) k -> r h k", r=P))
                keys.append(keys_tile)

        zeros = keep.tile([P, NTOK], BF16, name="zeros", align_bytes=64)
        nc.vector.memset(zeros[:], 0.0)
        ident = keep.tile([P, P], F32, name="ident", align_bytes=64)
        make_identity(nc, ident[:])
        eps = keep.tile([P, 1], F32, name="eps")
        nc.gpsimd.memset(eps[:], EPS)
        text_scales = keep.tile([P, 2, D], F32, name="text_scales", align_bytes=64)
        gain = keep.tile([P, PACK], F32, name="gain")
        bias_gain = keep.tile([P, PACK], F32, name="bias_gain")

        wq_pairs = keep.tile([P, PACK * D], BF16, name="wq_pairs", align_bytes=64)
        wq_codes = keep.tile([P, D], U32, name="wq_codes", align_bytes=64)
        wq_scales = keep.tile([P, D], U8, name="wq_scales", align_bytes=64)
        key_codes = keep.tile([P, B, S], U32, name="key_codes", align_bytes=64)
        key_scales = keep.tile([P, B, S], U8, name="key_scales", align_bytes=64)

        text_bf16, text_turned, text_pairs, text_mx = {}, {}, {}, {}
        q_banks, squares, affine_q = {}, {}, {}
        square_sums, rstd, rstd_spread = {}, {}, {}
        y_pairs, y_mx, score_banks, scores = {}, {}, {}, {}
        wq_turned, key_turned, key_pairs = {}, {}, {}

        def main_bank(shape):
            bank = psum.tile(shape, F32, name="main", bufs=4)
            return bank

        def keep_clock(bank, count=1):
            for n in range(count):
                nc.tensor.matmul(out=bank, lhsT=zeros[:, 0:P], rhs=zeros[:], start=True, stop=True)

        def turn_two_row_tiles(bank, row_tiles):
            for n, rows in enumerate(row_tiles):
                words = rows.bitcast(F32)
                for u in range(2):
                    nc.tensor.transpose(bank[:, n, u, :], words[:, u:WORDS:2], ident[:])

        def copy_pairs(copy, pairs, part, bank):
            dst = pairs[:].bitcast(F32)[:, 4 * P * part : 4 * P * (part + 1)]
            copy(out=dst.rearrange("p (n r u) -> p n r u", n=2, u=2), in_=bank[:].rearrange("p n u r -> p n r u"))

        def turn_wq(part):
            wq_turned[part] = main_bank([P, 2, 2, P])
            turn_two_row_tiles(wq_turned[part], [wq[:, 2 * part + n, :] for n in range(2)])

        def turn_keys(b):
            key_turned[b] = main_bank([P, 2, 2, P])
            turn_two_row_tiles(key_turned[b], [keys[b][:, h, :] for h in range(2)])

        def copy_keys(b):
            key_pairs[b] = work.tile([P, PACK * S], BF16, name="key_pairs", align_bytes=64)
            copy_pairs(nc.scalar.copy, key_pairs[b], 0, key_turned[b])

        def quantise_keys(b):
            nc.vector.quantize_mx(out=key_codes[:, b, :].bitcast(FP8X4), scales=key_scales[:, b, :], in_=key_pairs[b][:])

        def scale_text(i, half, parts=1):
            if not 0 <= i < NB:
                return
            if half == 0:
                text_bf16[i] = work.tile([P, NJ * D], BF16, name="text_bf16", bufs=4, align_bytes=64)
            flat_bytes = byte_tiles[i][:].rearrange("r j k -> r (j k)")
            flat_scales = text_scales[:].rearrange("r n k -> r (n k)")
            width = 2 * D // parts
            for part in range(parts):
                cols = slice(2 * D * half + width * part, 2 * D * half + width * (part + 1))
                nc.vector.tensor_tensor(
                    out=text_bf16[i][:, cols], in0=flat_bytes[:, cols].bitcast(FP8), in1=flat_scales[:, 0:width], op=ALU.mult
                )

        def turn_text(i, half, fill=True):
            if not 0 <= i < NB:
                return
            bank = psum.tile([P, 2, 2, P], F32, name="text_bank", bufs=2)
            text_turned[i, half] = bank
            if fill:
                keep_clock(bank[:].rearrange("p n u r -> p (n u r)"))
            turn_two_row_tiles(bank, [text_bf16[i][:, D * j : D * (j + 1)] for j in (2 * half, 2 * half + 1)])

        def copy_text(i, half):
            if not 0 <= i < NB:
                return
            if half == 0:
                text_pairs[i] = work.tile([P, PACK * NTOK], BF16, name="text_pairs", bufs=3, align_bytes=64)
            copy_pairs(nc.scalar.copy, text_pairs[i], half, text_turned[i, half])

        def quantise_text(i):
            if not 0 <= i < NB:
                return
            codes = work.tile([P, NTOK], U32, name="text_codes", bufs=3, align_bytes=64)
            scales = work.tile([P, NTOK], U8, name="text_mx_scales", bufs=3, align_bytes=64)
            nc.vector.quantize_mx(out=codes[:].bitcast(FP8X4), scales=scales[:], in_=text_pairs[i][:])
            text_mx[i] = (codes, scales)

        def project(i, t):
            if not 0 <= i < NB:
                return
            q_banks[i, t] = main_bank([P, NTOK])
            codes, scales = text_mx[i]
            cols = slice(P * t, P * (t + 1))
            nc.tensor.matmul_mx(
                out=q_banks[i, t][:],
                lhsT=wq_codes[:, cols].bitcast(FP8X4),
                lhsT_scale=wq_scales[:, cols],
                rhs=codes[:].bitcast(FP8X4),
                rhs_scale=scales[:],
                start=True,
                stop=True,
            )

        def square(i, t):
            if t == 0:
                squares[i] = work.tile([P, PACK, NTOK], F32, name="squares", align_bytes=64)
                affine_q[i] = work.tile([P, PACK, NTOK], F32, name="affine_q", bufs=3, align_bytes=64)
            nc.scalar.activation(out=squares[i][:, t, :], in_=q_banks[i, t][:], func=ACT.Square, bias=bias[:, t : t + 1])

        def apply_gain(i, t):
            nc.scalar.activation(
                out=affine_q[i][:, t, :],
                in_=q_banks[i, t][:],
                func=ACT.Identity,
                bias=bias_gain[:, t : t + 1],
                scale=gain[:, t : t + 1],
            )

        def square_and_gain(i, t):
            square(i, t)
            apply_gain(i, t)

        def sum_slices(i):
            if not 0 <= i < NB:
                return
            square_sums[i] = psum.tile([P, NJ, P], F32, name="sum_bank")
            for j in range(NJ):
                for t in range(PACK):
                    nc.tensor.matmul(
                        out=square_sums[i][:, j, :],
                        lhsT=squares[i][:, t, P * j : P * (j + 1)],
                        rhs=ident[:],
                        is_transpose=True,
                        start=(t == 0),
                        stop=(t == PACK - 1),
                    )

        def sum_features(i, parts=1):
            if not 0 <= i < NB:
                return
            rstd[i] = []
            n = NJ // parts
            for part in range(parts):
                total = work.tile([P, NJ], F32, name="total", bufs=4)
                nc.vector.tensor_reduce(
                    out=total[:, 0:n], in_=square_sums[i][:, n * part : n * (part + 1), :], axis=AX.X, op=ALU.add
                )
                root = work.tile([P, NJ], F32, name="root", bufs=4)
                rstd[i].append((total, root))

        def take_roots(i):
            if not 0 <= i < NB:
                return
            n = NJ // len(rstd[i])
            for total, root in rstd[i]:
                nc.scalar.activation(
                    out=root[:, 0:n], in_=total[:, 0:n], func=ACT.Abs_reciprocal_sqrt, scale=1.0 / D, bias=eps[:, 0:1]
                )

        def spread_roots(i):
            if not 0 <= i < NB:
                return
            rstd_spread[i] = psum.tile([P, NTOK], F32, name="root_bank")
            n = NJ // len(rstd[i])
            for j in range(NJ):
                root = rstd[i][j // n][1]
                column = root[:, j % n : j % n + 1]
                nc.tensor.transpose(rstd_spread[i][:, P * j : P * (j + 1)], column.to_broadcast([P, P]), ident[:])

        def normalise(i, lo=0, hi=NTOK):
            if not 0 <= i < NB:
                return
            if lo == 0:
                y_pairs[i] = work.tile([P, PACK * NTOK], BF16, name="y_pairs", align_bytes=64)
            roots = rstd_spread[i][:, lo:hi].rearrange("p (c n) -> p c n", n=GROUP).unsqueeze(2)
            nc.vector.tensor_tensor(
                out=y_pairs[i][:, PACK * lo : PACK * hi].rearrange("p (c n t) -> p c t n", n=GROUP, t=PACK),
                in0=affine_q[i][:, :, lo:hi].rearrange("p t (c n) -> p c t n", n=GROUP),
                in1=roots.to_broadcast([P, (hi - lo) // GROUP, PACK, GROUP]),
                op=ALU.mult,
            )

        def quantise_y(i, lo=0, hi=NTOK):
            if not 0 <= i < NB:
                return
            if lo == 0:
                codes = work.tile([P, NTOK], U32, name="y_codes", align_bytes=64)
                scales = work.tile([P, NTOK], U8, name="y_scales", align_bytes=64)
                y_mx[i] = (codes, scales)
            codes, scales = y_mx[i]
            nc.vector.quantize_mx(
                out=codes[:, lo:hi].bitcast(FP8X4), scales=scales[:, lo:hi], in_=y_pairs[i][:, PACK * lo : PACK * hi]
            )

        def score(i, half):
            if not 0 <= i < NB:
                return
            b = i // PER_B
            codes, scales = y_mx[i]
            bank = main_bank([P, 2, S])
            score_banks[i, half] = bank
            for n in range(2):
                cols = slice(P * (2 * half + n), P * (2 * half + n + 1))
                nc.tensor.matmul_mx(
                    out=bank[:, n, :],
                    lhsT=codes[:, cols].bitcast(FP8X4),
                    lhsT_scale=scales[:, cols],
                    rhs=key_codes[:, b, :].bitcast(FP8X4),
                    rhs_scale=key_scales[:, b, :],
                    start=True,
                    stop=True,
                )

        def store(i, half, on_vector=False):
            if not 0 <= i < NB:
                return
            if half == 0:
                scores[i] = work.tile([P, NJ, S], F32, name="scores", bufs=3, align_bytes=64)
            part = scores[i][:, 2 * half : 2 * half + 2, :]
            factor = 1.0 / D**0.5
            if on_vector:
                nc.vector.tensor_scalar(out=part, in0=score_banks[i, half][:], scalar1=factor, scalar2=None, op0=ALU.mult)
            else:
                nc.scalar.activation(out=part, in_=score_banks[i, half][:], func=ACT.Copy, scale=factor)
            dst = out_rows[NTOK * i : NTOK * (i + 1), :].rearrange("(r j) s -> r j s", j=NJ)
            if i == NB - 1:
                nc.sync.dma_start(out=dst[:, 2 * half : 2 * half + 2, :], in_=part)
            elif half == 1:
                nc.sync.dma_start(out=dst, in_=scores[i][:])

        idle_bank = psum.tile([P, NTOK], F32, name="root_bank")
        keep_clock(idle_bank[:], count=4)
        scale_bank = psum.tile([P, PACK, P], F32, name="sum_bank")
        for t in range(PACK):
            nc.tensor.transpose(scale_bank[:, t, :], scale_cols[:, t : t + 1].to_broadcast([P, P]), ident[:])
        for part, copy in enumerate((nc.scalar.copy, nc.vector.tensor_copy)):
            dst = text_scales[:, part, :].rearrange("p (n t) -> p n t", t=PACK)
            copy(out=dst, in_=scale_bank[:].rearrange("p t n -> p n t"))
        turn_wq(0)
        turn_wq(1)
        copy_pairs(nc.scalar.copy, wq_pairs, 0, wq_turned[0])
        copy_pairs(nc.scalar.copy, wq_pairs, 1, wq_turned[1])
        scale_text(0, 0, parts=2)
        scale_text(0, 1, parts=2)
        scale_text(1, 0)
        turn_text(0, 0, fill=False)
        turn_text(0, 1, fill=False)
        nc.vector.quantize_mx(out=wq_codes[:].bitcast(FP8X4), scales=wq_scales[:], in_=wq_pairs[:])
        nc.vector.tensor_copy(out=gain[:], in_=gain_bf16[:])
        nc.vector.tensor_mul(out=bias_gain[:], in0=bias[:], in1=gain_bf16[:])
        copy_text(0, 0)
        copy_text(0, 1)
        quantise_text(0)
        turn_text(1, 0, fill=False)
        project(0, 0)
        project(0, 1)
        idle_bank = psum.tile([P, NTOK], F32, name="sum_bank")
        keep_clock(idle_bank[:], count=4)
        project(0, 2)
        scale_text(1, 1)
        turn_text(1, 1, fill=False)
        scale_text(2, 0)
        scale_text(2, 1)

        for s in range(NB - 1):
            new_b = s % PER_B == 0
            copy_text(s + 1, 0)
            normalise(s - 2)
            if s > 0:
                project(s, 2)
            sum_slices(s - 1)
            score(s - 3, 0)
            sum_features(s - 1)
            square_and_gain(s, 0)
            square_and_gain(s, 1)
            turn_text(s + 2, 0)
            scale_text(s + 3, 0)
            copy_text(s + 1, 1)
            if new_b:
                turn_keys(s // PER_B)
            quantise_text(s + 1)
            square_and_gain(s, 2)
            score(s - 3, 1)
            take_roots(s - 1)
            if new_b:
                copy_keys(s // PER_B)
            project(s, 3)
            store(s - 3, 0)
            turn_text(s + 2, 1)
            spread_roots(s - 1)
            store(s - 3, 1, on_vector=not new_b)
            project(s + 1, 0)
            square_and_gain(s, 3)
            scale_text(s + 3, 1)
            quantise_y(s - 2)
            project(s + 1, 1)
            if new_b:
                quantise_keys(s // PER_B)

        s = NB - 1
        project(s, 2)
        project(s, 3)
        square(s, 0)
        square(s, 1)
        sum_slices(s - 1)
        normalise(s - 2)
        sum_features(s - 1)
        apply_gain(s, 0)
        apply_gain(s, 1)
        square(s, 2)
        square(s, 3)
        take_roots(s - 1)
        apply_gain(s, 2)
        apply_gain(s, 3)
        score(s - 3, 0)
        score(s - 3, 1)
        quantise_y(s - 2)
        sum_slices(s)
        spread_roots(s - 1)
        sum_features(s, parts=2)
        take_roots(s)
        store(s - 3, 0)
        store(s - 3, 1)
        normalise(s - 1)
        score(s - 2, 0)
        score(s - 2, 1)
        store(s - 2, 0)
        store(s - 2, 1)
        spread_roots(s)
        quantise_y(s - 1)
        normalise(s, 0, HALF)
        normalise(s, HALF, NTOK)
        score(s - 1, 0)
        score(s - 1, 1)
        store(s - 1, 0)
        store(s - 1, 1)
        quantise_y(s, 0, HALF)
        score(s, 0)
        store(s, 0)
        quantise_y(s, HALF, NTOK)
        score(s, 1)
        store(s, 1, on_vector=True)
